import numpy as np
import ml_dtypes

BF16 = ml_dtypes.bfloat16


def bf(x):
    return np.asarray(x, np.float32).astype(BF16)


def f32(x):
    return np.asarray(x, np.float32)


def f64(x):
    return np.asarray(x).astype(np.float64)


def striped(idx):
    return np.tile(idx.reshape(-1, 16).T, (8, 1))


D, S, N = 128, 1024, 256


def setup_inputs():
    return {"table": bf(np.random.standard_normal((D, S))), "wq": bf(1.25 * np.random.standard_normal((D, D)) / np.sqrt(D)), "wk": bf(1.25 * np.random.standard_normal((D, D)) / np.sqrt(D)), "wv": bf(2.0 * np.random.standard_normal((D, D)) / np.sqrt(D)), "offs": striped(np.random.permutation(S)[:N])}


def reference(table, wq, wk, wv, offs):
    idx = offs[:16].T.reshape(-1)
    xg = f64(table)[:, idx]
    q = f64(wq).T @ xg
    k = f64(wk).T @ xg
    v = f64(wv).T @ xg
    sc = (k.T @ q) / np.sqrt(D)
    e = np.exp(sc - sc.max(axis=0, keepdims=True))
    a = e / e.sum(axis=0, keepdims=True)
    return v @ a

@@ -1,0 +1,103 @@
+import math
+
+import concourse.mybir as mybir
+from concourse.masks import make_identity
+
+P = 128
+STORE = 1024
+N = 256
+BLOCKS = N // P
+BF16, F32, U16 = mybir.dt.bfloat16, mybir.dt.float32, mybir.dt.uint16
+EXP = mybir.ActivationFunctionType.Exp
+
+FLOPS = 3 * 2 * P * P * N + 2 * 2 * N * N * P
+
+
+def block(b):
+    return slice(b * P, (b + 1) * P)
+
+
+def tile_seqparallelattn_kernel(tc, table, wq, wk, wv, offs, out):
+    nc = tc.nc
+    with (
+        tc.tile_pool(name="held", bufs=1) as held,
+        tc.psum_pool(name="psum", bufs=8) as psum,
+    ):
+        offsets = held.tile([P, N // 16], U16, name="offsets")
+        nc.sync.dma_start(offsets[:], offs)
+        store = held.tile([P, STORE], BF16, name="store")
+        nc.sync.dma_start(store[:], table)
+        wq_sb = held.tile([P, P], BF16, name="wq_sb")
+        nc.scalar.dma_start(wq_sb[:], wq)
+        wk_sb = held.tile([P, P], BF16, name="wk_sb")
+        nc.scalar.dma_start(wk_sb[:], wk)
+        wv_sb = held.tile([P, P], BF16, name="wv_sb")
+        nc.scalar.dma_start(wv_sb[:], wv)
+
+        ident_bf = held.tile([P, P], BF16, name="ident_bf")
+        make_identity(nc, ident_bf[:])
+        ident_f32 = held.tile([P, P], F32, name="ident_f32")
+        make_identity(nc, ident_f32[:])
+        vT_ones = [held.tile([P, P + 1], BF16, name=f"vT_ones{i}") for i in range(BLOCKS)]
+        for i in range(BLOCKS):
+            nc.gpsimd.memset(vT_ones[i][:], 1.0)
+
+        q_acc = psum.tile([P, N], F32, name="q_acc", tag="bank")
+        nc.tensor.matmul(q_acc[:], wq_sb[:], store[:].indirect(offsets[:]), start=True, stop=True)
+        k_acc = psum.tile([P, N], F32, name="k_acc", tag="bank")
+        nc.tensor.matmul(k_acc[:], wk_sb[:], store[:].indirect(offsets[:]), start=True, stop=True)
+        v_acc = psum.tile([P, N], F32, name="v_acc", tag="bank")
+        nc.tensor.matmul(v_acc[:], wv_sb[:], store[:].indirect(offsets[:]), start=True, stop=True)
+        q_bf = held.tile([P, N], BF16, name="q_bf")
+        nc.vector.tensor_copy(q_bf[:], q_acc[:])
+        k_bf = held.tile([P, N], BF16, name="k_bf")
+        nc.scalar.copy(k_bf[:], k_acc[:])
+        v_bf = held.tile([P, N], BF16, name="v_bf")
+        nc.scalar.copy(v_bf[:], v_acc[:])
+
+        neg_max = held.tile([P, BLOCKS], BF16, name="neg_max")
+        for j in range(BLOCKS):
+            by_query = psum.tile([P, N], F32, name="by_query", tag="bank")
+            nc.tensor.matmul(by_query[:], q_bf[:, block(j)], k_bf[:], start=True, stop=True)
+            with nc.allow_low_precision(reason="the softmax's shift may be a rounded maximum"):
+                nc.vector.reduce_max(neg_max[:, j : j + 1], by_query[:], axis=mybir.AxisListType.X, negate=True)
+
+        by_key = [psum.tile([P, N], F32, name=f"by_key{i}", tag="bank") for i in range(BLOCKS)]
+        for i in range(BLOCKS):
+            nc.tensor.matmul(by_key[i][:], k_bf[:, block(i)], q_bf[:], start=True, stop=False)
+        for j in range(BLOCKS):
+            for i in range(BLOCKS):
+                nc.tensor.matmul(
+                    by_key[i][:, block(j)],
+                    neg_max[:, j : j + 1].to_broadcast([P, P]),
+                    ident_bf[:],
+                    start=False,
+                    stop=(j == BLOCKS - 1),
+                )
+
+        for i in range(BLOCKS):
+            vT_acc = psum.tile([P, P], BF16, name="vT_acc", tag="bank")
+            nc.tensor.transpose(vT_acc[:], v_bf[:, block(i)], ident_bf[:])
+            nc.vector.tensor_copy(vT_ones[i][:, 0:P], vT_acc[:])
+
+        weights = [held.tile([P, N], BF16, name=f"weights{i}") for i in range(BLOCKS)]
+        for i in range(BLOCKS):
+            nc.scalar.activation(weights[i][:], by_key[i][:], EXP, scale=1.0 / math.sqrt(P))
+
+        mixed = [psum.tile([P, P + 1], F32, name=f"mixed{j}", tag="bank") for j in range(BLOCKS)]
+        for i in range(BLOCKS):
+            for j in range(BLOCKS):
+                nc.tensor.matmul(
+                    mixed[j][:], weights[i][:, block(j)], vT_ones[i][:], start=(i == 0), stop=(i == BLOCKS - 1)
+                )
+
+        for j in range(BLOCKS):
+            inv_sum = held.tile([P, 1], F32, name=f"inv_sum{j}")
+            nc.vector.reciprocal(inv_sum[:], mixed[j][:, P : P + 1])
+            by_query_out = held.tile([P, P], F32, name=f"by_query_out{j}")
+            nc.vector.tensor_scalar_mul(by_query_out[:], mixed[j][:, 0:P], inv_sum[:])
+            out_acc = psum.tile([P, P], F32, name="out_acc", tag="bank")
+            nc.tensor.transpose(out_acc[:], by_query_out[:], ident_f32[:])
+            out_sb = held.tile([P, P], F32, name=f"out_sb{j}")
+            nc.vector.tensor_copy(out_sb[:], out_acc[:])
+            nc.sync.dma_start(out[:, block(j)], out_sb[:])

@@ -62,42 +62,42 @@ def tile_seqparallelattn_kernel(tc, table, wq, wk, wv, offs, out):
             with nc.allow_low_precision(reason="the softmax's shift may be a rounded maximum"):
                 nc.vector.reduce_max(neg_max[:, j : j + 1], by_query[:], axis=mybir.AxisListType.X, negate=True)
 
-        by_key = [psum.tile([P, N], F32, name=f"by_key{i}", tag="bank") for i in range(BLOCKS)]
+        by_key = [
+            [psum.tile([P, P], F32, name=f"by_key{i}{j}", tag="bank") for j in range(BLOCKS)] for i in range(BLOCKS)
+        ]
         for i in range(BLOCKS):
-            nc.tensor.matmul(by_key[i][:], k_bf[:, block(i)], q_bf[:], start=True, stop=False)
-        for j in range(BLOCKS):
-            for i in range(BLOCKS):
-                nc.tensor.matmul(
-                    by_key[i][:, block(j)],
-                    neg_max[:, j : j + 1].to_broadcast([P, P]),
-                    ident_bf[:],
-                    start=False,
-                    stop=(j == BLOCKS - 1),
-                )
+            for j in range(BLOCKS):
+                nc.tensor.matmul(by_key[i][j][:], k_bf[:, block(i)], q_bf[:, block(j)], start=True, stop=False)
 
         for i in range(BLOCKS):
             vT_acc = psum.tile([P, P], BF16, name="vT_acc", tag="bank")
             nc.tensor.transpose(vT_acc[:], v_bf[:, block(i)], ident_bf[:])
             nc.vector.tensor_copy(vT_ones[i][:, 0:P], vT_acc[:])
 
-        weights = [held.tile([P, N], BF16, name=f"weights{i}") for i in range(BLOCKS)]
-        for i in range(BLOCKS):
-            nc.scalar.activation(weights[i][:], by_key[i][:], EXP, scale=1.0 / math.sqrt(P))
-
-        mixed = [psum.tile([P, P + 1], F32, name=f"mixed{j}", tag="bank") for j in range(BLOCKS)]
-        for i in range(BLOCKS):
-            for j in range(BLOCKS):
-                nc.tensor.matmul(
-                    mixed[j][:], weights[i][:, block(j)], vT_ones[i][:], start=(i == 0), stop=(i == BLOCKS - 1)
-                )
-
         for j in range(BLOCKS):
+            weights = held.tile([P, BLOCKS, P], BF16, name=f"weights{j}")
+            for i in range(BLOCKS):
+                nc.tensor.matmul(
+                    by_key[i][j][:], neg_max[:, j : j + 1].to_broadcast([P, P]), ident_bf[:], start=False, stop=True
+                )
+                nc.scalar.activation(weights[:, i, :], by_key[i][j][:], EXP, scale=1.0 / math.sqrt(P))
+
+            mixed = psum.tile([P, P + 1], F32, name="mixed", tag="bank")
+            for i in range(BLOCKS):
+                nc.tensor.matmul(mixed[:], weights[:, i, :], vT_ones[i][:], start=(i == 0), stop=(i == BLOCKS - 1))
+
             inv_sum = held.tile([P, 1], F32, name=f"inv_sum{j}")
-            nc.vector.reciprocal(inv_sum[:], mixed[j][:, P : P + 1])
+            nc.vector.reciprocal(inv_sum[:], mixed[:, P : P + 1])
             by_query_out = held.tile([P, P], F32, name=f"by_query_out{j}")
-            nc.vector.tensor_scalar_mul(by_query_out[:], mixed[j][:, 0:P], inv_sum[:])
             out_acc = psum.tile([P, P], F32, name="out_acc", tag="bank")
-            nc.tensor.transpose(out_acc[:], by_query_out[:], ident_f32[:])
             out_sb = held.tile([P, P], F32, name=f"out_sb{j}")
-            nc.vector.tensor_copy(out_sb[:], out_acc[:])
-            nc.sync.dma_start(out[:, block(j)], out_sb[:])
+            if j == 0:
+                nc.vector.tensor_scalar_mul(by_query_out[:], mixed[:, 0:P], inv_sum[:])
+                nc.tensor.transpose(out_acc[:], by_query_out[:], ident_f32[:])
+                nc.vector.tensor_copy(out_sb[:], out_acc[:])
+                nc.sync.dma_start(out[:, block(j)], out_sb[:])
+            else:
+                nc.scalar.mul(by_query_out[:], mixed[:, 0:P], inv_sum[:])
+                nc.tensor.transpose(out_acc[:], by_query_out[:], ident_f32[:])
+                nc.scalar.copy(out_sb[:], out_acc[:])
+                nc.scalar.dma_start(out[:, block(j)], out_sb[:])

@@ -9,6 +9,8 @@ N = 256
 BLOCKS = N // P
 BF16, F32, U16 = mybir.dt.bfloat16, mybir.dt.float32, mybir.dt.uint16
 EXP = mybir.ActivationFunctionType.Exp
+WARM_COLUMNS = 128
+WARM_MATMULS = 16
 
 FLOPS = 3 * 2 * P * P * N + 2 * 2 * N * N * P
 
@@ -33,6 +35,12 @@ def tile_seqparallelattn_kernel(tc, table, wq, wk, wv, offs, out):
         nc.scalar.dma_start(wk_sb[:], wk)
         wv_sb = held.tile([P, P], BF16, name="wv_sb")
         nc.scalar.dma_start(wv_sb[:], wv)
+
+        zeros = held.tile([P, WARM_COLUMNS], BF16, name="zeros")
+        nc.gpsimd.memset(zeros[:], 0.0)
+        warm_acc = psum.tile([P, WARM_COLUMNS], F32, name="warm_acc", tag="bank")
+        for repeat in range(WARM_MATMULS):
+            nc.tensor.matmul(warm_acc[:], zeros[:, 0:P], zeros[:], start=True, stop=True)
 
         ident_bf = held.tile([P, P], BF16, name="ident_bf")
         make_identity(nc, ident_bf[:])
@@ -74,30 +82,36 @@ def tile_seqparallelattn_kernel(tc, table, wq, wk, wv, offs, out):
             nc.tensor.transpose(vT_acc[:], v_bf[:, block(i)], ident_bf[:])
             nc.vector.tensor_copy(vT_ones[i][:, 0:P], vT_acc[:])
 
+
+        weights = [held.tile([P, BLOCKS, P], BF16, name=f"weights{j}") for j in range(BLOCKS)]
         for j in range(BLOCKS):
-            weights = held.tile([P, BLOCKS, P], BF16, name=f"weights{j}")
             for i in range(BLOCKS):
                 nc.tensor.matmul(
                     by_key[i][j][:], neg_max[:, j : j + 1].to_broadcast([P, P]), ident_bf[:], start=False, stop=True
                 )
-                nc.scalar.activation(weights[:, i, :], by_key[i][j][:], EXP, scale=1.0 / math.sqrt(P))
+                nc.scalar.activation(weights[j][:, i, :], by_key[i][j][:], EXP, scale=1.0 / math.sqrt(P))
 
+        by_query_out = [held.tile([P, P], F32, name=f"by_query_out{j}") for j in range(BLOCKS)]
+        for j in range(BLOCKS):
             mixed = psum.tile([P, P + 1], F32, name="mixed", tag="bank")
             for i in range(BLOCKS):
-                nc.tensor.matmul(mixed[:], weights[:, i, :], vT_ones[i][:], start=(i == 0), stop=(i == BLOCKS - 1))
-
+                nc.tensor.matmul(
+                    mixed[:], weights[j][:, i, :], vT_ones[i][:], start=(i == 0), stop=(i == BLOCKS - 1)
+                )
             inv_sum = held.tile([P, 1], F32, name=f"inv_sum{j}")
             nc.vector.reciprocal(inv_sum[:], mixed[:, P : P + 1])
-            by_query_out = held.tile([P, P], F32, name=f"by_query_out{j}")
+            if j == 0:
+                nc.vector.tensor_scalar_mul(by_query_out[j][:], mixed[:, 0:P], inv_sum[:])
+            else:
+                nc.scalar.mul(by_query_out[j][:], mixed[:, 0:P], inv_sum[:])
+
+        for j in range(BLOCKS):
             out_acc = psum.tile([P, P], F32, name="out_acc", tag="bank")
+            nc.tensor.transpose(out_acc[:], by_query_out[j][:], ident_f32[:])
             out_sb = held.tile([P, P], F32, name=f"out_sb{j}")
             if j == 0:
-                nc.vector.tensor_scalar_mul(by_query_out[:], mixed[:, 0:P], inv_sum[:])
-                nc.tensor.transpose(out_acc[:], by_query_out[:], ident_f32[:])
                 nc.vector.tensor_copy(out_sb[:], out_acc[:])
                 nc.sync.dma_start(out[:, block(j)], out_sb[:])
             else:
-                nc.scalar.mul(by_query_out[:], mixed[:, 0:P], inv_sum[:])
-                nc.tensor.transpose(out_acc[:], by_query_out[:], ident_f32[:])
                 nc.scalar.copy(out_sb[:], out_acc[:])
                 nc.scalar.dma_start(out[:, block(j)], out_sb[:])

@@ -28,13 +28,13 @@ def tile_seqparallelattn_kernel(tc, table, wq, wk, wv, offs, out):
         offsets = held.tile([P, N // 16], U16, name="offsets")
         nc.sync.dma_start(offsets[:], offs)
         store = held.tile([P, STORE], BF16, name="store")
-        nc.sync.dma_start(store[:], table)
-        wq_sb = held.tile([P, P], BF16, name="wq_sb")
-        nc.scalar.dma_start(wq_sb[:], wq)
+        nc.scalar.dma_start(store[:], table)
         wk_sb = held.tile([P, P], BF16, name="wk_sb")
-        nc.scalar.dma_start(wk_sb[:], wk)
+        nc.sync.dma_start(wk_sb[:], wk)
+        wq_sb = held.tile([P, P], BF16, name="wq_sb")
+        nc.sync.dma_start(wq_sb[:], wq)
         wv_sb = held.tile([P, P], BF16, name="wv_sb")
-        nc.scalar.dma_start(wv_sb[:], wv)
+        nc.sync.dma_start(wv_sb[:], wv)
 
         zeros = held.tile([P, WARM_COLUMNS], BF16, name="zeros")
         nc.gpsimd.memset(zeros[:], 0.0)
@@ -50,25 +50,31 @@ def tile_seqparallelattn_kernel(tc, table, wq, wk, wv, offs, out):
         for i in range(BLOCKS):
             nc.gpsimd.memset(vT_ones[i][:], 1.0)
 
-        q_acc = psum.tile([P, N], F32, name="q_acc", tag="bank")
-        nc.tensor.matmul(q_acc[:], wq_sb[:], store[:].indirect(offsets[:]), start=True, stop=True)
         k_acc = psum.tile([P, N], F32, name="k_acc", tag="bank")
         nc.tensor.matmul(k_acc[:], wk_sb[:], store[:].indirect(offsets[:]), start=True, stop=True)
-        v_acc = psum.tile([P, N], F32, name="v_acc", tag="bank")
-        nc.tensor.matmul(v_acc[:], wv_sb[:], store[:].indirect(offsets[:]), start=True, stop=True)
-        q_bf = held.tile([P, N], BF16, name="q_bf")
-        nc.vector.tensor_copy(q_bf[:], q_acc[:])
         k_bf = held.tile([P, N], BF16, name="k_bf")
         nc.scalar.copy(k_bf[:], k_acc[:])
+        q_bf = held.tile([P, N], BF16, name="q_bf")
+        for j in range(BLOCKS):
+            q_acc = psum.tile([P, P], F32, name="q_acc", tag="bank")
+            piece = offsets[:, j * (P // 16) : (j + 1) * (P // 16)]
+            nc.tensor.matmul(q_acc[:], wq_sb[:], store[:].indirect(piece), start=True, stop=True)
+            nc.vector.tensor_copy(q_bf[:, block(j)], q_acc[:])
+        v_acc = psum.tile([P, N], F32, name="v_acc", tag="bank")
+        nc.tensor.matmul(v_acc[:], wv_sb[:], store[:].indirect(offsets[:]), start=True, stop=True)
         v_bf = held.tile([P, N], BF16, name="v_bf")
         nc.scalar.copy(v_bf[:], v_acc[:])
 
         neg_max = held.tile([P, BLOCKS], BF16, name="neg_max")
         for j in range(BLOCKS):
-            by_query = psum.tile([P, N], F32, name="by_query", tag="bank")
+            by_query = psum.tile([P, N], BF16, name="by_query", tag="bank")
             nc.tensor.matmul(by_query[:], q_bf[:, block(j)], k_bf[:], start=True, stop=True)
+            negated = held.tile([P, N], BF16, name=f"negated{j}")
             with nc.allow_low_precision(reason="the softmax's shift may be a rounded maximum"):
-                nc.vector.reduce_max(neg_max[:, j : j + 1], by_query[:], axis=mybir.AxisListType.X, negate=True)
+                nc.vector.tensor_scalar(
+                    negated[:], by_query[:], -1.0, None, mybir.AluOpType.mult, mybir.AluOpType.min,
+                    accum_out=neg_max[:, j : j + 1],
+                )
 
         by_key = [
             [psum.tile([P, P], F32, name=f"by_key{i}{j}", tag="bank") for j in range(BLOCKS)] for i in range(BLOCKS)

@@ -9,7 +9,6 @@ N = 256
 BLOCKS = N // P
 BF16, F32, U16 = mybir.dt.bfloat16, mybir.dt.float32, mybir.dt.uint16
 EXP = mybir.ActivationFunctionType.Exp
-WARM_COLUMNS = 128
 WARM_MATMULS = 16
 
 FLOPS = 3 * 2 * P * P * N + 2 * 2 * N * N * P
@@ -36,19 +35,21 @@ def tile_seqparallelattn_kernel(tc, table, wq, wk, wv, offs, out):
         wv_sb = held.tile([P, P], BF16, name="wv_sb")
         nc.sync.dma_start(wv_sb[:], wv)
 
-        zeros = held.tile([P, WARM_COLUMNS], BF16, name="zeros")
-        nc.gpsimd.memset(zeros[:], 0.0)
-        warm_acc = psum.tile([P, WARM_COLUMNS], F32, name="warm_acc", tag="bank")
+        zeros = held.tile([P, P], BF16, name="zeros")
+        nc.vector.memset(zeros[:], 0.0)
+        warm_acc = psum.tile([P, P], F32, name="warm_acc", tag="bank")
         for repeat in range(WARM_MATMULS):
-            nc.tensor.matmul(warm_acc[:], zeros[:, 0:P], zeros[:], start=True, stop=True)
+            nc.tensor.matmul(warm_acc[:], zeros[:], zeros[:], start=True, stop=True)
 
         ident_bf = held.tile([P, P], BF16, name="ident_bf")
-        make_identity(nc, ident_bf[:])
+        nc.vector.memset(ident_bf[:], 0.0)
+        make_identity(nc, ident_bf[:], nomemset=True)
         ident_f32 = held.tile([P, P], F32, name="ident_f32")
-        make_identity(nc, ident_f32[:])
+        nc.vector.memset(ident_f32[:], 0.0)
+        make_identity(nc, ident_f32[:], nomemset=True)
         vT_ones = [held.tile([P, P + 1], BF16, name=f"vT_ones{i}") for i in range(BLOCKS)]
         for i in range(BLOCKS):
-            nc.gpsimd.memset(vT_ones[i][:], 1.0)
+            nc.vector.memset(vT_ones[i][:, P : P + 1], 1.0)
 
         k_acc = psum.tile([P, N], F32, name="k_acc", tag="bank")
         nc.tensor.matmul(k_acc[:], wk_sb[:], store[:].indirect(offsets[:]), start=True, stop=True)

@@ -47,9 +47,8 @@ def tile_seqparallelattn_kernel(tc, table, wq, wk, wv, offs, out):
         ident_f32 = held.tile([P, P], F32, name="ident_f32")
         nc.vector.memset(ident_f32[:], 0.0)
         make_identity(nc, ident_f32[:], nomemset=True)
-        vT_ones = [held.tile([P, P + 1], BF16, name=f"vT_ones{i}") for i in range(BLOCKS)]
-        for i in range(BLOCKS):
-            nc.vector.memset(vT_ones[i][:, P : P + 1], 1.0)
+        ones = held.tile([P, 1], BF16, name="ones")
+        nc.vector.memset(ones[:], 1.0)
 
         k_acc = psum.tile([P, N], F32, name="k_acc", tag="bank")
         nc.tensor.matmul(k_acc[:], wk_sb[:], store[:].indirect(offsets[:]), start=True, stop=True)
@@ -84,10 +83,11 @@ def tile_seqparallelattn_kernel(tc, table, wq, wk, wv, offs, out):
             for j in range(BLOCKS):
                 nc.tensor.matmul(by_key[i][j][:], k_bf[:, block(i)], q_bf[:, block(j)], start=True, stop=False)
 
+        vT = [held.tile([P, P], BF16, name=f"vT{i}") for i in range(BLOCKS)]
         for i in range(BLOCKS):
             vT_acc = psum.tile([P, P], BF16, name="vT_acc", tag="bank")
             nc.tensor.transpose(vT_acc[:], v_bf[:, block(i)], ident_bf[:])
-            nc.vector.tensor_copy(vT_ones[i][:, 0:P], vT_acc[:])
+            nc.vector.tensor_copy(vT[i][:], vT_acc[:])
 
 
         weights = [held.tile([P, BLOCKS, P], BF16, name=f"weights{j}") for j in range(BLOCKS)]
@@ -98,27 +98,23 @@ def tile_seqparallelattn_kernel(tc, table, wq, wk, wv, offs, out):
                 )
                 nc.scalar.activation(weights[j][:, i, :], by_key[i][j][:], EXP, scale=1.0 / math.sqrt(P))
 
-        by_query_out = [held.tile([P, P], F32, name=f"by_query_out{j}") for j in range(BLOCKS)]
+        inv_sum = [held.tile([P, 1], F32, name=f"inv_sum{j}") for j in range(BLOCKS)]
+        mixed_sb = [held.tile([P, P], F32, name=f"mixed_sb{j}") for j in range(BLOCKS)]
         for j in range(BLOCKS):
-            mixed = psum.tile([P, P + 1], F32, name="mixed", tag="bank")
+            sums = psum.tile([P, 1], F32, name="sums", tag="bank")
+            mixed = psum.tile([P, P], F32, name="mixed", tag="bank")
             for i in range(BLOCKS):
-                nc.tensor.matmul(
-                    mixed[:], weights[j][:, i, :], vT_ones[i][:], start=(i == 0), stop=(i == BLOCKS - 1)
-                )
-            inv_sum = held.tile([P, 1], F32, name=f"inv_sum{j}")
-            nc.vector.reciprocal(inv_sum[:], mixed[:, P : P + 1])
+                nc.tensor.matmul(sums[:], weights[j][:, i, :], ones[:], start=(i == 0), stop=(i == BLOCKS - 1))
+                nc.tensor.matmul(mixed[:], vT[i][:], weights[j][:, i, :], start=(i == 0), stop=(i == BLOCKS - 1))
+            nc.vector.reciprocal(inv_sum[j][:], sums[:])
             if j == 0:
-                nc.vector.tensor_scalar_mul(by_query_out[j][:], mixed[:, 0:P], inv_sum[:])
+                nc.vector.tensor_copy(mixed_sb[j][:], mixed[:])
             else:
-                nc.scalar.mul(by_query_out[j][:], mixed[:, 0:P], inv_sum[:])
+                nc.scalar.copy(mixed_sb[j][:], mixed[:])
 
         for j in range(BLOCKS):
-            out_acc = psum.tile([P, P], F32, name="out_acc", tag="bank")
-            nc.tensor.transpose(out_acc[:], by_query_out[j][:], ident_f32[:])
+            inv_rows = psum.tile([P, P], F32, name="inv_rows", tag="bank")
+            nc.tensor.transpose(inv_rows[:], inv_sum[j][:].to_broadcast([P, P]), ident_f32[:])
             out_sb = held.tile([P, P], F32, name=f"out_sb{j}")
-            if j == 0:
-                nc.vector.tensor_copy(out_sb[:], out_acc[:])
-                nc.sync.dma_start(out[:, block(j)], out_sb[:])
-            else:
-                nc.scalar.copy(out_sb[:], out_acc[:])
-                nc.scalar.dma_start(out[:, block(j)], out_sb[:])
+            nc.vector.tensor_mul(out_sb[:], inv_rows[:], mixed_sb[j][:])
+            nc.sync.dma_start(out[:, block(j)], out_sb[:])

@@ -24,12 +24,12 @@ def tile_seqparallelattn_kernel(tc, table, wq, wk, wv, offs, out):
         tc.tile_pool(name="held", bufs=1) as held,
         tc.psum_pool(name="psum", bufs=8) as psum,
     ):
+        store = held.tile([P, STORE], BF16, name="store")
+        nc.sync.dma_start(store[:], table)
+        wk_sb = held.tile([P, P], BF16, name="wk_sb")
+        nc.scalar.dma_start(wk_sb[:], wk)
         offsets = held.tile([P, N // 16], U16, name="offsets")
         nc.sync.dma_start(offsets[:], offs)
-        store = held.tile([P, STORE], BF16, name="store")
-        nc.scalar.dma_start(store[:], table)
-        wk_sb = held.tile([P, P], BF16, name="wk_sb")
-        nc.sync.dma_start(wk_sb[:], wk)
         wq_sb = held.tile([P, P], BF16, name="wq_sb")
         nc.sync.dma_start(wq_sb[:], wq)
         wv_sb = held.tile([P, P], BF16, name="wv_sb")

import math

import concourse.mybir as mybir
from concourse.masks import make_identity

P = 128
STORE = 1024
N = 256
BLOCKS = N // P
BF16, F32, U16 = mybir.dt.bfloat16, mybir.dt.float32, mybir.dt.uint16
EXP = mybir.ActivationFunctionType.Exp
WARM_MATMULS = 16

FLOPS = 3 * 2 * P * P * N + 2 * 2 * N * N * P


def block(b):
    return slice(b * P, (b + 1) * P)


def tile_seqparallelattn_kernel(tc, table, wq, wk, wv, offs, out):
    nc = tc.nc
    with (
        tc.tile_pool(name="held", bufs=1) as held,
        tc.psum_pool(name="psum", bufs=8) as psum,
    ):
        store = held.tile([P, STORE], BF16, name="store")
        nc.sync.dma_start(store[:], table)
        wk_sb = held.tile([P, P], BF16, name="wk_sb")
        nc.scalar.dma_start(wk_sb[:], wk)
        offsets = held.tile([P, N // 16], U16, name="offsets")
        nc.sync.dma_start(offsets[:], offs)
        wq_sb = held.tile([P, P], BF16, name="wq_sb")
        nc.sync.dma_start(wq_sb[:], wq)
        wv_sb = held.tile([P, P], BF16, name="wv_sb")
        nc.sync.dma_start(wv_sb[:], wv)

        zeros = held.tile([P, P], BF16, name="zeros")
        nc.vector.memset(zeros[:], 0.0)
        warm_acc = psum.tile([P, P], F32, name="warm_acc", tag="bank")
        for repeat in range(WARM_MATMULS):
            nc.tensor.matmul(warm_acc[:], zeros[:], zeros[:], start=True, stop=True)

        ident_bf = held.tile([P, P], BF16, name="ident_bf")
        nc.vector.memset(ident_bf[:], 0.0)
        make_identity(nc, ident_bf[:], nomemset=True)
        ident_f32 = held.tile([P, P], F32, name="ident_f32")
        nc.vector.memset(ident_f32[:], 0.0)
        make_identity(nc, ident_f32[:], nomemset=True)
        ones = held.tile([P, 1], BF16, name="ones")
        nc.vector.memset(ones[:], 1.0)

        k_acc = psum.tile([P, N], F32, name="k_acc", tag="bank")
        nc.tensor.matmul(k_acc[:], wk_sb[:], store[:].indirect(offsets[:]), start=True, stop=True)
        k_bf = held.tile([P, N], BF16, name="k_bf")
        nc.scalar.copy(k_bf[:], k_acc[:])
        q_bf = held.tile([P, N], BF16, name="q_bf")
        for j in range(BLOCKS):
            q_acc = psum.tile([P, P], F32, name="q_acc", tag="bank")
            piece = offsets[:, j * (P // 16) : (j + 1) * (P // 16)]
            nc.tensor.matmul(q_acc[:], wq_sb[:], store[:].indirect(piece), start=True, stop=True)
            nc.vector.tensor_copy(q_bf[:, block(j)], q_acc[:])
        v_acc = psum.tile([P, N], F32, name="v_acc", tag="bank")
        nc.tensor.matmul(v_acc[:], wv_sb[:], store[:].indirect(offsets[:]), start=True, stop=True)
        v_bf = held.tile([P, N], BF16, name="v_bf")
        nc.scalar.copy(v_bf[:], v_acc[:])

        neg_max = held.tile([P, BLOCKS], BF16, name="neg_max")
        for j in range(BLOCKS):
            by_query = psum.tile([P, N], BF16, name="by_query", tag="bank")
            nc.tensor.matmul(by_query[:], q_bf[:, block(j)], k_bf[:], start=True, stop=True)
            negated = held.tile([P, N], BF16, name=f"negated{j}")
            with nc.allow_low_precision(reason="the softmax's shift may be a rounded maximum"):
                nc.vector.tensor_scalar(
                    negated[:], by_query[:], -1.0, None, mybir.AluOpType.mult, mybir.AluOpType.min,
                    accum_out=neg_max[:, j : j + 1],
                )

        by_key = [
            [psum.tile([P, P], F32, name=f"by_key{i}{j}", tag="bank") for j in range(BLOCKS)] for i in range(BLOCKS)
        ]
        for i in range(BLOCKS):
            for j in range(BLOCKS):
                nc.tensor.matmul(by_key[i][j][:], k_bf[:, block(i)], q_bf[:, block(j)], start=True, stop=False)

        vT = [held.tile([P, P], BF16, name=f"vT{i}") for i in range(BLOCKS)]
        for i in range(BLOCKS):
            vT_acc = psum.tile([P, P], BF16, name="vT_acc", tag="bank")
            nc.tensor.transpose(vT_acc[:], v_bf[:, block(i)], ident_bf[:])
            nc.vector.tensor_copy(vT[i][:], vT_acc[:])


        weights = [held.tile([P, BLOCKS, P], BF16, name=f"weights{j}") for j in range(BLOCKS)]
        for j in range(BLOCKS):
            for i in range(BLOCKS):
                nc.tensor.matmul(
                    by_key[i][j][:], neg_max[:, j : j + 1].to_broadcast([P, P]), ident_bf[:], start=False, stop=True
                )
                nc.scalar.activation(weights[j][:, i, :], by_key[i][j][:], EXP, scale=1.0 / math.sqrt(P))

        inv_sum = [held.tile([P, 1], F32, name=f"inv_sum{j}") for j in range(BLOCKS)]
        mixed_sb = [held.tile([P, P], F32, name=f"mixed_sb{j}") for j in range(BLOCKS)]
        for j in range(BLOCKS):
            sums = psum.tile([P, 1], F32, name="sums", tag="bank")
            mixed = psum.tile([P, P], F32, name="mixed", tag="bank")
            for i in range(BLOCKS):
                nc.tensor.matmul(sums[:], weights[j][:, i, :], ones[:], start=(i == 0), stop=(i == BLOCKS - 1))
                nc.tensor.matmul(mixed[:], vT[i][:], weights[j][:, i, :], start=(i == 0), stop=(i == BLOCKS - 1))
            nc.vector.reciprocal(inv_sum[j][:], sums[:])
            if j == 0:
                nc.vector.tensor_copy(mixed_sb[j][:], mixed[:])
            else:
                nc.scalar.copy(mixed_sb[j][:], mixed[:])

        for j in range(BLOCKS):
            inv_rows = psum.tile([P, P], F32, name="inv_rows", tag="bank")
            nc.tensor.transpose(inv_rows[:], inv_sum[j][:].to_broadcast([P, P]), ident_f32[:])
            out_sb = held.tile([P, P], F32, name=f"out_sb{j}")
            nc.vector.tensor_mul(out_sb[:], inv_rows[:], mixed_sb[j][:])
            nc.sync.dma_start(out[:, block(j)], out_sb[:])
